import numpy as np
import ml_dtypes

BF16 = ml_dtypes.bfloat16


def bf(x):
    return np.asarray(x, np.float32).astype(BF16)


def f32(x):
    return np.asarray(x, np.float32)


def f64(x):
    return np.asarray(x).astype(np.float64)


def striped(idx):
    return np.tile(idx.reshape(-1, 16).T, (8, 1))


S, D, H, KV, C, B, T, N = 256, 128, 128, 256, 128, 8, 16, 2048


def setup_inputs():
    return {
        "table": bf(np.random.standard_normal((S, D))),
        "w": bf(np.random.standard_normal((D, H)) / np.sqrt(D)),
        "pe_b": f32(0.5 * np.random.standard_normal((H, 1))),
        "feat": bf(np.random.standard_normal((C, B * T))),
        "q_w": bf(np.random.standard_normal((C, H)) / np.sqrt(C)),
        "kv_w": bf(np.random.standard_normal((C, KV)) / np.sqrt(C)),
        "blank_k": f32(np.random.standard_normal((H, 1))),
        "blank_v": f32(np.random.standard_normal((H, 1))),
        "offs": striped(np.concatenate([np.random.permutation(S) for _ in range(N // S)])),
    }


def reference(table, w, pe_b, feat, q_w, kv_w, blank_k, blank_v, offs):
    idx = offs[:16].T.reshape(-1)
    pos = (f64(w).T @ f64(table)[idx].T + f64(pe_b)).reshape(H, B, T, T)
    q = (f64(q_w).T @ f64(feat)).reshape(H, B, T)
    kv = f64(kv_w).T @ f64(feat)
    key = kv[:H].reshape(H, B, T)
    val = kv[H:].reshape(H, B, T)
    score = q[:, :, :, None] * key[:, :, None, :] + pos
    blank = q * f64(blank_k)[:, :, None]
    top = np.maximum(score.max(axis=-1), blank)
    e = np.exp(score - top[..., None])
    eb = np.exp(blank - top)
    den = e.sum(axis=-1) + eb
    res = ((e * val[:, :, None, :]).sum(axis=-1) + eb * f64(blank_v)[:, :, None]) / den
    return res.reshape(H, B * T)

@@ -1,0 +1,142 @@
+import concourse.mybir as mybir
+from concourse.masks import make_identity
+
+BF16, F32, U16 = mybir.dt.bfloat16, mybir.dt.float32, mybir.dt.uint16
+ADD, SUB, MULT, MAX = (
+    mybir.AluOpType.add,
+    mybir.AluOpType.subtract,
+    mybir.AluOpType.mult,
+    mybir.AluOpType.max,
+)
+EXP = mybir.ActivationFunctionType.Exp
+X = mybir.AxisListType.X
+
+P = 128
+ROWS = 256
+B, T = 8, 16
+KEYS = T + 1
+PIECE = T * T
+N = B * PIECE
+GROUP = 2
+STEPS = B // GROUP
+
+FLOPS = 2 * P * P * N + 2 * P * (3 * P) * (B * T)
+
+
+def tile_clusterattention_old_kernel(
+    tc, table, w, pe_b, feat, q_w, kv_w, blank_k, blank_v, offs, out
+):
+    nc = tc.nc
+    with (
+        tc.tile_pool(name="held", bufs=1) as held,
+        tc.tile_pool(name="work", bufs=STEPS) as work,
+        tc.psum_pool(name="setup_psum", bufs=1) as setup_psum,
+        tc.psum_pool(name="pos_psum", bufs=STEPS) as pos_psum,
+    ):
+        table_rows = [held.tile([P, P], BF16, name=f"table_rows{b}") for b in range(2)]
+        offsets = held.tile([P, N // 16], U16, name="offsets")
+        w_sb = held.tile([P, P], BF16, name="w_sb")
+        feat_sb = held.tile([P, B * T], BF16, name="feat_sb")
+        q_w_sb = held.tile([P, P], BF16, name="q_w_sb")
+        kv_w_sb = held.tile([P, 2 * P], BF16, name="kv_w_sb")
+        pe_b_sb = held.tile([P, 1], F32, name="pe_b_sb")
+        blank_k_sb = held.tile([P, 1], F32, name="blank_k_sb")
+        blank_v_sb = held.tile([P, 1], F32, name="blank_v_sb")
+        nc.sync.dma_start(table_rows[0][:], table[0:P, :])
+        nc.scalar.dma_start(table_rows[1][:], table[P : 2 * P, :])
+        nc.sync.dma_start(offsets[:], offs)
+        nc.scalar.dma_start(kv_w_sb[:], kv_w)
+        nc.sync.dma_start(feat_sb[:], feat)
+        nc.scalar.dma_start(q_w_sb[:], q_w)
+        nc.sync.dma_start(w_sb[:], w)
+        nc.scalar.dma_start(blank_k_sb[:], blank_k)
+        nc.sync.dma_start(pe_b_sb[:], pe_b)
+        nc.scalar.dma_start(blank_v_sb[:], blank_v)
+
+        warm = held.tile([P, 1], F32, name="warm")
+        nc.vector.memset(warm[:], 0.0)
+        nc.scalar.activation(out=warm[:], in_=warm[:], func=EXP)
+
+        ident = held.tile([P, P], BF16, name="ident")
+        make_identity(nc, ident[:])
+        window_ps = setup_psum.tile([P, ROWS], BF16, name="window_ps")
+        for b in range(2):
+            nc.tensor.transpose(window_ps[:, b * P : (b + 1) * P], table_rows[b][:], ident[:])
+        window = held.tile([P, ROWS], BF16, name="window")
+        nc.vector.tensor_copy(window[:], window_ps[:])
+
+        qkv_ps = setup_psum.tile([P, 3, B, T], F32, name="qkv_ps")
+        for i, weights in enumerate((q_w_sb[:], kv_w_sb[:, 0:P], kv_w_sb[:, P : 2 * P])):
+            nc.tensor.matmul(
+                qkv_ps[:, i].rearrange("h a t -> h (a t)"), weights, feat_sb[:], start=True, stop=True
+            )
+        q_key = held.tile([P, 2, B, T], F32, name="q_key")
+        nc.vector.tensor_copy(q_key[:], qkv_ps[:, 0:2])
+        q, key = q_key[:, 0], q_key[:, 1]
+        val = held.tile([P, B, KEYS], F32, name="val")
+        nc.vector.tensor_copy(val[:, :, 0:T], qkv_ps[:, 2])
+        nc.vector.tensor_copy(val[:, :, T:KEYS], blank_v_sb[:].unsqueeze(1).to_broadcast([P, B, 1]))
+
+        res = held.tile([P, B, T], F32, name="res")
+        for step in range(STEPS):
+            a0 = step * GROUP
+            a1 = a0 + GROUP
+
+            pos = pos_psum.tile([P, GROUP, T, T], F32, name="pos")
+            for g in range(GROUP):
+                piece = offsets[:, (a0 + g) * (PIECE // 16) : (a0 + g + 1) * (PIECE // 16)]
+                nc.tensor.matmul(
+                    pos[:, g].rearrange("h t u -> h (t u)"),
+                    w_sb[:],
+                    window[:].indirect(piece),
+                    start=True,
+                    stop=True,
+                )
+
+            pairs = [P, GROUP, T, T]
+            prod = work.tile(pairs, F32, name="prod")
+            nc.vector.tensor_tensor(
+                out=prod[:],
+                in0=q[:, a0:a1, :].unsqueeze(3).to_broadcast(pairs),
+                in1=key[:, a0:a1, :].unsqueeze(2).to_broadcast(pairs),
+                op=MULT,
+            )
+            with_blank = [P, GROUP, T, KEYS]
+            score = work.tile(with_blank, F32, name="score")
+            nc.vector.tensor_tensor(out=score[:, :, :, 0:T], in0=pos[:], in1=prod[:], op=ADD)
+            nc.vector.tensor_scalar(
+                out=score[:, :, :, T:KEYS],
+                in0=q[:, a0:a1, :].unsqueeze(3),
+                scalar1=blank_k_sb[:, 0:1],
+                scalar2=pe_b_sb[:, 0:1],
+                op0=MULT,
+                op1=SUB,
+            )
+
+            neg_top = work.tile([P, GROUP, T], F32, name="neg_top")
+            nc.vector.tensor_reduce(out=neg_top[:], in_=score[:], axis=X, op=MAX, negate=True)
+            shifted = work.tile(with_blank, F32, name="shifted")
+            nc.vector.tensor_tensor(
+                out=shifted[:],
+                in0=score[:],
+                in1=neg_top[:].unsqueeze(3).to_broadcast(with_blank),
+                op=ADD,
+            )
+            e = work.tile(with_blank, F32, name="e")
+            nc.scalar.activation(out=e[:], in_=shifted[:], func=EXP)
+            den = work.tile([P, GROUP, T], F32, name="den")
+            nc.vector.tensor_reduce(out=den[:], in_=e[:], axis=X, op=ADD)
+            weighted = work.tile(with_blank, F32, name="weighted")
+            nc.vector.tensor_tensor(
+                out=weighted[:],
+                in0=e[:],
+                in1=val[:, a0:a1, :].unsqueeze(2).to_broadcast(with_blank),
+                op=MULT,
+            )
+            num = work.tile([P, GROUP, T], F32, name="num")
+            nc.vector.tensor_reduce(out=num[:], in_=weighted[:], axis=X, op=ADD)
+            inv_den = work.tile([P, GROUP, T], F32, name="inv_den")
+            nc.vector.reciprocal(inv_den[:], den[:])
+            nc.vector.tensor_tensor(out=res[:, a0:a1, :], in0=num[:], in1=inv_den[:], op=MULT)
+
+        nc.sync.dma_start(out, res[:].rearrange("h a t -> h (a t)"))

@@ -17,8 +17,7 @@ B, T = 8, 16
 KEYS = T + 1
 PIECE = T * T
 N = B * PIECE
-GROUP = 2
-STEPS = B // GROUP
+BANK = 2
 
 FLOPS = 2 * P * P * N + 2 * P * (3 * P) * (B * T)
 
@@ -29,9 +28,7 @@ def tile_clusterattention_old_kernel(
     nc = tc.nc
     with (
         tc.tile_pool(name="held", bufs=1) as held,
-        tc.tile_pool(name="work", bufs=STEPS) as work,
-        tc.psum_pool(name="setup_psum", bufs=1) as setup_psum,
-        tc.psum_pool(name="pos_psum", bufs=STEPS) as pos_psum,
+        tc.psum_pool(name="psum", bufs=1) as psum,
     ):
         table_rows = [held.tile([P, P], BF16, name=f"table_rows{b}") for b in range(2)]
         offsets = held.tile([P, N // 16], U16, name="offsets")
@@ -44,14 +41,14 @@ def tile_clusterattention_old_kernel(
         blank_v_sb = held.tile([P, 1], F32, name="blank_v_sb")
         nc.sync.dma_start(table_rows[0][:], table[0:P, :])
         nc.scalar.dma_start(table_rows[1][:], table[P : 2 * P, :])
-        nc.sync.dma_start(offsets[:], offs)
-        nc.scalar.dma_start(kv_w_sb[:], kv_w)
         nc.sync.dma_start(feat_sb[:], feat)
-        nc.scalar.dma_start(q_w_sb[:], q_w)
+        nc.scalar.dma_start(kv_w_sb[:], kv_w)
+        nc.sync.dma_start(q_w_sb[:], q_w)
+        nc.sync.dma_start(offsets[:], offs)
         nc.sync.dma_start(w_sb[:], w)
-        nc.scalar.dma_start(blank_k_sb[:], blank_k)
+        nc.sync.dma_start(blank_k_sb[:], blank_k)
         nc.sync.dma_start(pe_b_sb[:], pe_b)
-        nc.scalar.dma_start(blank_v_sb[:], blank_v)
+        nc.sync.dma_start(blank_v_sb[:], blank_v)
 
         warm = held.tile([P, 1], F32, name="warm")
         nc.vector.memset(warm[:], 0.0)
@@ -59,84 +56,73 @@ def tile_clusterattention_old_kernel(
 
         ident = held.tile([P, P], BF16, name="ident")
         make_identity(nc, ident[:])
-        window_ps = setup_psum.tile([P, ROWS], BF16, name="window_ps")
+        window_ps = psum.tile([P, ROWS], BF16, name="window_ps")
         for b in range(2):
             nc.tensor.transpose(window_ps[:, b * P : (b + 1) * P], table_rows[b][:], ident[:])
         window = held.tile([P, ROWS], BF16, name="window")
         nc.vector.tensor_copy(window[:], window_ps[:])
 
-        qkv_ps = setup_psum.tile([P, 3, B, T], F32, name="qkv_ps")
+        qkv_ps = psum.tile([P, 3, B, T], F32, name="qkv_ps")
         for i, weights in enumerate((q_w_sb[:], kv_w_sb[:, 0:P], kv_w_sb[:, P : 2 * P])):
             nc.tensor.matmul(
                 qkv_ps[:, i].rearrange("h a t -> h (a t)"), weights, feat_sb[:], start=True, stop=True
             )
         q_key = held.tile([P, 2, B, T], F32, name="q_key")
-        nc.vector.tensor_copy(q_key[:], qkv_ps[:, 0:2])
+        nc.scalar.copy(q_key[:], qkv_ps[:, 0:2])
         q, key = q_key[:, 0], q_key[:, 1]
         val = held.tile([P, B, KEYS], F32, name="val")
-        nc.vector.tensor_copy(val[:, :, 0:T], qkv_ps[:, 2])
-        nc.vector.tensor_copy(val[:, :, T:KEYS], blank_v_sb[:].unsqueeze(1).to_broadcast([P, B, 1]))
+        nc.scalar.copy(val[:, :, 0:T], qkv_ps[:, 2])
+        nc.scalar.copy(val[:, :, T:KEYS], blank_v_sb[:].unsqueeze(1).to_broadcast([P, B, 1]))
 
+        pos = [psum.tile([P, BANK, T, T], F32, name=f"pos{i}") for i in range(B // BANK)]
+        for a in range(B):
+            nc.tensor.matmul(
+                pos[a // BANK][:, a % BANK].rearrange("h t u -> h (t u)"),
+                w_sb[:],
+                window[:].indirect(offsets[:, a * (PIECE // 16) : (a + 1) * (PIECE // 16)]),
+                start=True,
+                stop=True,
+            )
+
+        prod = held.tile([P, B, T, T], F32, name="prod")
+        score = held.tile([P, B, T, KEYS], F32, name="score")
+        neg_top = held.tile([P, B, T], F32, name="neg_top")
+        e = held.tile([P, B, T, KEYS], F32, name="e")
+        weighted = held.tile([P, B, T, KEYS], F32, name="weighted")
+        den = held.tile([P, B, T], F32, name="den")
+        num = held.tile([P, B, T], F32, name="num")
+        inv_den = held.tile([P, B, T], F32, name="inv_den")
         res = held.tile([P, B, T], F32, name="res")
-        for step in range(STEPS):
-            a0 = step * GROUP
-            a1 = a0 + GROUP
 
-            pos = pos_psum.tile([P, GROUP, T, T], F32, name="pos")
-            for g in range(GROUP):
-                piece = offsets[:, (a0 + g) * (PIECE // 16) : (a0 + g + 1) * (PIECE // 16)]
-                nc.tensor.matmul(
-                    pos[:, g].rearrange("h t u -> h (t u)"),
-                    w_sb[:],
-                    window[:].indirect(piece),
-                    start=True,
-                    stop=True,
+        nc.vector.tensor_scalar(
+            out=score[:, :, :, T:KEYS],
+            in0=q.unsqueeze(3),
+            scalar1=blank_k_sb[:, 0:1],
+            scalar2=pe_b_sb[:, 0:1],
+            op0=MULT,
+            op1=SUB,
+        )
+
+        for a in range(B):
+            for t in range(T):
+                nc.scalar.mul(prod[:, a, t, :], key[:, a, :], q[:, a, t : t + 1])
+            nc.vector.tensor_tensor(
+                out=score[:, a, :, 0:T], in0=pos[a // BANK][:, a % BANK], in1=prod[:, a], op=ADD
+            )
+            nc.vector.tensor_reduce(out=neg_top[:, a], in_=score[:, a], axis=X, op=MAX, negate=True)
+            for t in range(T):
+                nc.scalar.activation(
+                    out=e[:, a, t, :], in_=score[:, a, t, :], func=EXP, bias=neg_top[:, a, t : t + 1]
                 )
-
-            pairs = [P, GROUP, T, T]
-            prod = work.tile(pairs, F32, name="prod")
-            nc.vector.tensor_tensor(
-                out=prod[:],
-                in0=q[:, a0:a1, :].unsqueeze(3).to_broadcast(pairs),
-                in1=key[:, a0:a1, :].unsqueeze(2).to_broadcast(pairs),
+            nc.vector.tensor_reduce(out=den[:, a], in_=e[:, a], axis=X, op=ADD)
+            nc.gpsimd.tensor_tensor(
+                out=weighted[:, a],
+                in0=e[:, a],
+                in1=val[:, a : a + 1, :].to_broadcast([P, T, KEYS]),
                 op=MULT,
             )
-            with_blank = [P, GROUP, T, KEYS]
-            score = work.tile(with_blank, F32, name="score")
-            nc.vector.tensor_tensor(out=score[:, :, :, 0:T], in0=pos[:], in1=prod[:], op=ADD)
-            nc.vector.tensor_scalar(
-                out=score[:, :, :, T:KEYS],
-                in0=q[:, a0:a1, :].unsqueeze(3),
-                scalar1=blank_k_sb[:, 0:1],
-                scalar2=pe_b_sb[:, 0:1],
-                op0=MULT,
-                op1=SUB,
-            )
-
-            neg_top = work.tile([P, GROUP, T], F32, name="neg_top")
-            nc.vector.tensor_reduce(out=neg_top[:], in_=score[:], axis=X, op=MAX, negate=True)
-            shifted = work.tile(with_blank, F32, name="shifted")
-            nc.vector.tensor_tensor(
-                out=shifted[:],
-                in0=score[:],
-                in1=neg_top[:].unsqueeze(3).to_broadcast(with_blank),
-                op=ADD,
-            )
-            e = work.tile(with_blank, F32, name="e")
-            nc.scalar.activation(out=e[:], in_=shifted[:], func=EXP)
-            den = work.tile([P, GROUP, T], F32, name="den")
-            nc.vector.tensor_reduce(out=den[:], in_=e[:], axis=X, op=ADD)
-            weighted = work.tile(with_blank, F32, name="weighted")
-            nc.vector.tensor_tensor(
-                out=weighted[:],
-                in0=e[:],
-                in1=val[:, a0:a1, :].unsqueeze(2).to_broadcast(with_blank),
-                op=MULT,
-            )
-            num = work.tile([P, GROUP, T], F32, name="num")
-            nc.vector.tensor_reduce(out=num[:], in_=weighted[:], axis=X, op=ADD)
-            inv_den = work.tile([P, GROUP, T], F32, name="inv_den")
-            nc.vector.reciprocal(inv_den[:], den[:])
-            nc.vector.tensor_tensor(out=res[:, a0:a1, :], in0=num[:], in1=inv_den[:], op=MULT)
+            nc.vector.tensor_reduce(out=num[:, a], in_=weighted[:, a], axis=X, op=ADD)
+            nc.vector.reciprocal(inv_den[:, a], den[:, a])
+            nc.vector.tensor_tensor(out=res[:, a], in0=num[:, a], in1=inv_den[:, a], op=MULT)
 
         nc.sync.dma_start(out, res[:].rearrange("h a t -> h (a t)"))

@@ -2,9 +2,8 @@ import concourse.mybir as mybir
 from concourse.masks import make_identity
 
 BF16, F32, U16 = mybir.dt.bfloat16, mybir.dt.float32, mybir.dt.uint16
-ADD, SUB, MULT, MAX = (
+ADD, MULT, MAX = (
     mybir.AluOpType.add,
-    mybir.AluOpType.subtract,
     mybir.AluOpType.mult,
     mybir.AluOpType.max,
 )
@@ -17,7 +16,7 @@ B, T = 8, 16
 KEYS = T + 1
 PIECE = T * T
 N = B * PIECE
-BANK = 2
+PAIR = 2
 
 FLOPS = 2 * P * P * N + 2 * P * (3 * P) * (B * T)
 
@@ -30,7 +29,7 @@ def tile_clusterattention_old_kernel(
         tc.tile_pool(name="held", bufs=1) as held,
         tc.psum_pool(name="psum", bufs=1) as psum,
     ):
-        table_rows = [held.tile([P, P], BF16, name=f"table_rows{b}") for b in range(2)]
+        table_rows = held.tile([P, ROWS // P, P], BF16, name="table_rows")
         offsets = held.tile([P, N // 16], U16, name="offsets")
         w_sb = held.tile([P, P], BF16, name="w_sb")
         feat_sb = held.tile([P, B * T], BF16, name="feat_sb")
@@ -39,14 +38,13 @@ def tile_clusterattention_old_kernel(
         pe_b_sb = held.tile([P, 1], F32, name="pe_b_sb")
         blank_k_sb = held.tile([P, 1], F32, name="blank_k_sb")
         blank_v_sb = held.tile([P, 1], F32, name="blank_v_sb")
-        nc.sync.dma_start(table_rows[0][:], table[0:P, :])
-        nc.scalar.dma_start(table_rows[1][:], table[P : 2 * P, :])
-        nc.sync.dma_start(feat_sb[:], feat)
-        nc.scalar.dma_start(kv_w_sb[:], kv_w)
-        nc.sync.dma_start(q_w_sb[:], q_w)
+        nc.sync.dma_start(table_rows[:], table.rearrange("(b p) d -> p b d", p=P))
+        nc.scalar.dma_start(feat_sb[:], feat)
+        nc.sync.dma_start(kv_w_sb[:], kv_w)
+        nc.scalar.dma_start(q_w_sb[:], q_w)
         nc.sync.dma_start(offsets[:], offs)
+        nc.scalar.dma_start(blank_k_sb[:], blank_k)
         nc.sync.dma_start(w_sb[:], w)
-        nc.sync.dma_start(blank_k_sb[:], blank_k)
         nc.sync.dma_start(pe_b_sb[:], pe_b)
         nc.sync.dma_start(blank_v_sb[:], blank_v)
 
@@ -57,8 +55,8 @@ def tile_clusterattention_old_kernel(
         ident = held.tile([P, P], BF16, name="ident")
         make_identity(nc, ident[:])
         window_ps = psum.tile([P, ROWS], BF16, name="window_ps")
-        for b in range(2):
-            nc.tensor.transpose(window_ps[:, b * P : (b + 1) * P], table_rows[b][:], ident[:])
+        for b in range(ROWS // P):
+            nc.tensor.transpose(window_ps[:, b * P : (b + 1) * P], table_rows[:, b, :], ident[:])
         window = held.tile([P, ROWS], BF16, name="window")
         nc.vector.tensor_copy(window[:], window_ps[:])
 
@@ -67,25 +65,35 @@ def tile_clusterattention_old_kernel(
             nc.tensor.matmul(
                 qkv_ps[:, i].rearrange("h a t -> h (a t)"), weights, feat_sb[:], start=True, stop=True
             )
-        q_key = held.tile([P, 2, B, T], F32, name="q_key")
-        nc.scalar.copy(q_key[:], qkv_ps[:, 0:2])
-        q, key = q_key[:, 0], q_key[:, 1]
+        q = held.tile([P, B, T], F32, name="q")
+        key = held.tile([P, B, KEYS], F32, name="key")
         val = held.tile([P, B, KEYS], F32, name="val")
+        nc.scalar.copy(q[:], qkv_ps[:, 0])
+        nc.scalar.copy(key[:, :, 0:T], qkv_ps[:, 1])
+        nc.scalar.copy(key[:, :, T:KEYS], blank_k_sb[:].unsqueeze(1).to_broadcast([P, B, 1]))
         nc.scalar.copy(val[:, :, 0:T], qkv_ps[:, 2])
         nc.scalar.copy(val[:, :, T:KEYS], blank_v_sb[:].unsqueeze(1).to_broadcast([P, B, 1]))
 
-        pos = [psum.tile([P, BANK, T, T], F32, name=f"pos{i}") for i in range(B // BANK)]
+        pos = [psum.tile([P, PAIR, T, T], F32, name=f"pos{i}") for i in range(B // PAIR)]
         for a in range(B):
             nc.tensor.matmul(
-                pos[a // BANK][:, a % BANK].rearrange("h t u -> h (t u)"),
+                pos[a // PAIR][:, a % PAIR].rearrange("h t u -> h (t u)"),
                 w_sb[:],
                 window[:].indirect(offsets[:, a * (PIECE // 16) : (a + 1) * (PIECE // 16)]),
                 start=True,
                 stop=True,
             )
 
-        prod = held.tile([P, B, T, T], F32, name="prod")
         score = held.tile([P, B, T, KEYS], F32, name="score")
+        for a in range(0, B, PAIR):
+            engine = nc.vector if a == 0 else nc.gpsimd
+            engine.tensor_tensor(
+                out=score[:, a : a + PAIR],
+                in0=q[:, a : a + PAIR, :].unsqueeze(3).to_broadcast([P, PAIR, T, KEYS]),
+                in1=key[:, a : a + PAIR, :].unsqueeze(2).to_broadcast([P, PAIR, T, KEYS]),
+                op=MULT,
+            )
+
         neg_top = held.tile([P, B, T], F32, name="neg_top")
         e = held.tile([P, B, T, KEYS], F32, name="e")
         weighted = held.tile([P, B, T, KEYS], F32, name="weighted")
@@ -94,28 +102,25 @@ def tile_clusterattention_old_kernel(
         inv_den = held.tile([P, B, T], F32, name="inv_den")
         res = held.tile([P, B, T], F32, name="res")
 
-        nc.vector.tensor_scalar(
-            out=score[:, :, :, T:KEYS],
-            in0=q.unsqueeze(3),
-            scalar1=blank_k_sb[:, 0:1],
-            scalar2=pe_b_sb[:, 0:1],
-            op0=MULT,
-            op1=SUB,
-        )
-
         for a in range(B):
-            for t in range(T):
-                nc.scalar.mul(prod[:, a, t, :], key[:, a, :], q[:, a, t : t + 1])
-            nc.vector.tensor_tensor(
-                out=score[:, a, :, 0:T], in0=pos[a // BANK][:, a % BANK], in1=prod[:, a], op=ADD
+            nc.vector.scalar_tensor_tensor(
+                out=score[:, a, :, 0:T],
+                in0=pos[a // PAIR][:, a % PAIR],
+                scalar=pe_b_sb[:, 0:1],
+                in1=score[:, a, :, 0:T],
+                op0=ADD,
+                op1=ADD,
             )
             nc.vector.tensor_reduce(out=neg_top[:, a], in_=score[:, a], axis=X, op=MAX, negate=True)
             for t in range(T):
                 nc.scalar.activation(
                     out=e[:, a, t, :], in_=score[:, a, t, :], func=EXP, bias=neg_top[:, a, t : t + 1]
                 )
+
+        for a in range(B):
             nc.vector.tensor_reduce(out=den[:, a], in_=e[:, a], axis=X, op=ADD)
-            nc.gpsimd.tensor_tensor(
+            engine = nc.gpsimd if a < B - 1 else nc.vector
+            engine.tensor_tensor(
                 out=weighted[:, a],
                 in0=e[:, a],
                 in1=val[:, a : a + 1, :].to_broadcast([P, T, KEYS]),

@@ -60,18 +60,24 @@ def tile_clusterattention_old_kernel(
         window = held.tile([P, ROWS], BF16, name="window")
         nc.vector.tensor_copy(window[:], window_ps[:])
 
-        qkv_ps = psum.tile([P, 3, B, T], F32, name="qkv_ps")
-        for i, weights in enumerate((q_w_sb[:], kv_w_sb[:, 0:P], kv_w_sb[:, P : 2 * P])):
+        q_ps = psum.tile([P, B, T], F32, name="q_ps")
+        key_ps = psum.tile([P, B, T], F32, name="key_ps")
+        val_ps = psum.tile([P, B, T], F32, name="val_ps")
+        for product, weights in (
+            (q_ps, q_w_sb[:]),
+            (key_ps, kv_w_sb[:, 0:P]),
+            (val_ps, kv_w_sb[:, P : 2 * P]),
+        ):
             nc.tensor.matmul(
-                qkv_ps[:, i].rearrange("h a t -> h (a t)"), weights, feat_sb[:], start=True, stop=True
+                product[:].rearrange("h a t -> h (a t)"), weights, feat_sb[:], start=True, stop=True
             )
         q = held.tile([P, B, T], F32, name="q")
         key = held.tile([P, B, KEYS], F32, name="key")
         val = held.tile([P, B, KEYS], F32, name="val")
-        nc.scalar.copy(q[:], qkv_ps[:, 0])
-        nc.scalar.copy(key[:, :, 0:T], qkv_ps[:, 1])
+        nc.scalar.copy(key[:, :, 0:T], key_ps[:])
         nc.scalar.copy(key[:, :, T:KEYS], blank_k_sb[:].unsqueeze(1).to_broadcast([P, B, 1]))
-        nc.scalar.copy(val[:, :, 0:T], qkv_ps[:, 2])
+        nc.scalar.copy(q[:], q_ps[:])
+        nc.scalar.copy(val[:, :, 0:T], val_ps[:])
         nc.scalar.copy(val[:, :, T:KEYS], blank_v_sb[:].unsqueeze(1).to_broadcast([P, B, 1]))
 
         pos = [psum.tile([P, PAIR, T, T], F32, name=f"pos{i}") for i in range(B // PAIR)]
@@ -86,10 +92,10 @@ def tile_clusterattention_old_kernel(
 
         score = held.tile([P, B, T, KEYS], F32, name="score")
         for a in range(0, B, PAIR):
-            engine = nc.vector if a == 0 else nc.gpsimd
+            engine, q_of = (nc.vector, q_ps) if a == 0 else (nc.gpsimd, q)
             engine.tensor_tensor(
                 out=score[:, a : a + PAIR],
-                in0=q[:, a : a + PAIR, :].unsqueeze(3).to_broadcast([P, PAIR, T, KEYS]),
+                in0=q_of[:, a : a + PAIR, :].unsqueeze(3).to_broadcast([P, PAIR, T, KEYS]),
                 in1=key[:, a : a + PAIR, :].unsqueeze(2).to_broadcast([P, PAIR, T, KEYS]),
                 op=MULT,
             )
@@ -128,6 +134,6 @@ def tile_clusterattention_old_kernel(
             )
             nc.vector.tensor_reduce(out=num[:, a], in_=weighted[:, a], axis=X, op=ADD)
             nc.vector.reciprocal(inv_den[:, a], den[:, a])
-            nc.vector.tensor_tensor(out=res[:, a], in0=num[:, a], in1=inv_den[:, a], op=MULT)
+        nc.vector.tensor_tensor(out=res[:], in0=num[:], in1=inv_den[:], op=MULT)
 
         nc.sync.dma_start(out, res[:].rearrange("h a t -> h (a t)"))

@@ -16,6 +16,7 @@ B, T = 8, 16
 KEYS = T + 1
 PIECE = T * T
 N = B * PIECE
+LAST = 2
 PAIR = 2
 
 FLOPS = 2 * P * P * N + 2 * P * (3 * P) * (B * T)
@@ -123,17 +124,19 @@ def tile_clusterattention_old_kernel(
                     out=e[:, a, t, :], in_=score[:, a, t, :], func=EXP, bias=neg_top[:, a, t : t + 1]
                 )
 
-        for a in range(B):
-            nc.vector.tensor_reduce(out=den[:, a], in_=e[:, a], axis=X, op=ADD)
-            engine = nc.gpsimd if a < B - 1 else nc.vector
+        blocks = [(a, 0, T) for a in range(B - LAST)]
+        blocks += [(a, t0, t0 + T // 2) for a in range(B - LAST, B) for t0 in (0, T // 2)]
+        for a, t0, t1 in blocks:
+            engine = nc.gpsimd if a < B - LAST else nc.vector
             engine.tensor_tensor(
-                out=weighted[:, a],
-                in0=e[:, a],
-                in1=val[:, a : a + 1, :].to_broadcast([P, T, KEYS]),
+                out=weighted[:, a, t0:t1],
+                in0=e[:, a, t0:t1],
+                in1=val[:, a : a + 1, :].to_broadcast([P, t1 - t0, KEYS]),
                 op=MULT,
             )
-            nc.vector.tensor_reduce(out=num[:, a], in_=weighted[:, a], axis=X, op=ADD)
-            nc.vector.reciprocal(inv_den[:, a], den[:, a])
+            nc.vector.tensor_reduce(out=den[:, a, t0:t1], in_=e[:, a, t0:t1], axis=X, op=ADD)
+            nc.vector.tensor_reduce(out=num[:, a, t0:t1], in_=weighted[:, a, t0:t1], axis=X, op=ADD)
+            nc.vector.reciprocal(inv_den[:, a, t0:t1], den[:, a, t0:t1])
         nc.vector.tensor_tensor(out=res[:], in0=num[:], in1=inv_den[:], op=MULT)
 
         nc.sync.dma_start(out, res[:].rearrange("h a t -> h (a t)"))

@@ -109,34 +109,49 @@ def tile_clusterattention_old_kernel(
         inv_den = held.tile([P, B, T], F32, name="inv_den")
         res = held.tile([P, B, T], F32, name="res")
 
-        for a in range(B):
+        steps = [(a, a + 1) for a in range(PAIR)] + [(a, a + PAIR) for a in range(PAIR, B, PAIR)]
+        for a0, a1 in steps:
             nc.vector.scalar_tensor_tensor(
-                out=score[:, a, :, 0:T],
-                in0=pos[a // PAIR][:, a % PAIR],
+                out=score[:, a0:a1, :, 0:T],
+                in0=pos[a0 // PAIR][:, a0 % PAIR : a0 % PAIR + a1 - a0],
                 scalar=pe_b_sb[:, 0:1],
-                in1=score[:, a, :, 0:T],
+                in1=score[:, a0:a1, :, 0:T],
                 op0=ADD,
                 op1=ADD,
             )
-            nc.vector.tensor_reduce(out=neg_top[:, a], in_=score[:, a], axis=X, op=MAX, negate=True)
-            for t in range(T):
-                nc.scalar.activation(
-                    out=e[:, a, t, :], in_=score[:, a, t, :], func=EXP, bias=neg_top[:, a, t : t + 1]
-                )
+            nc.vector.tensor_reduce(out=neg_top[:, a0:a1], in_=score[:, a0:a1], axis=X, op=MAX, negate=True)
+            for a in range(a0, a1):
+                for t in range(T):
+                    nc.scalar.activation(
+                        out=e[:, a, t, :], in_=score[:, a, t, :], func=EXP, bias=neg_top[:, a, t : t + 1]
+                    )
 
-        blocks = [(a, 0, T) for a in range(B - LAST)]
-        blocks += [(a, t0, t0 + T // 2) for a in range(B - LAST, B) for t0 in (0, T // 2)]
-        for a, t0, t1 in blocks:
-            engine = nc.gpsimd if a < B - LAST else nc.vector
-            engine.tensor_tensor(
-                out=weighted[:, a, t0:t1],
-                in0=e[:, a, t0:t1],
-                in1=val[:, a : a + 1, :].to_broadcast([P, t1 - t0, KEYS]),
-                op=MULT,
-            )
-            nc.vector.tensor_reduce(out=den[:, a, t0:t1], in_=e[:, a, t0:t1], axis=X, op=ADD)
-            nc.vector.tensor_reduce(out=num[:, a, t0:t1], in_=weighted[:, a, t0:t1], axis=X, op=ADD)
-            nc.vector.reciprocal(inv_den[:, a, t0:t1], den[:, a, t0:t1])
+        early = slice(0, B - LAST)
+        for a0 in range(0, B - LAST, PAIR):
+            pair = slice(a0, a0 + PAIR)
+            for a in range(a0, a0 + PAIR):
+                nc.gpsimd.tensor_tensor(
+                    out=weighted[:, a],
+                    in0=e[:, a],
+                    in1=val[:, a : a + 1, :].to_broadcast([P, T, KEYS]),
+                    op=MULT,
+                )
+            nc.vector.tensor_reduce(out=den[:, pair], in_=e[:, pair], axis=X, op=ADD)
+            nc.vector.tensor_reduce(out=num[:, pair], in_=weighted[:, pair], axis=X, op=ADD)
+        nc.vector.reciprocal(inv_den[:, early], den[:, early])
+        late = slice(B - LAST, B)
+        for a in range(B - LAST, B):
+            for t0 in (0, T // 2):
+                half = slice(t0, t0 + T // 2)
+                nc.vector.tensor_tensor(
+                    out=weighted[:, a, half],
+                    in0=e[:, a, half],
+                    in1=val[:, a : a + 1, :].to_broadcast([P, T // 2, KEYS]),
+                    op=MULT,
+                )
+                nc.vector.tensor_reduce(out=den[:, a, half], in_=e[:, a, half], axis=X, op=ADD)
+                nc.vector.tensor_reduce(out=num[:, a, half], in_=weighted[:, a, half], axis=X, op=ADD)
+        nc.vector.reciprocal(inv_den[:, late], den[:, late])
         nc.vector.tensor_tensor(out=res[:], in0=num[:], in1=inv_den[:], op=MULT)
 
         nc.sync.dma_start(out, res[:].rearrange("h a t -> h (a t)"))

@@ -16,7 +16,6 @@ B, T = 8, 16
 KEYS = T + 1
 PIECE = T * T
 N = B * PIECE
-LAST = 2
 PAIR = 2
 
 FLOPS = 2 * P * P * N + 2 * P * (3 * P) * (B * T)
@@ -126,8 +125,7 @@ def tile_clusterattention_old_kernel(
                         out=e[:, a, t, :], in_=score[:, a, t, :], func=EXP, bias=neg_top[:, a, t : t + 1]
                     )
 
-        early = slice(0, B - LAST)
-        for a0 in range(0, B - LAST, PAIR):
+        for a0 in range(0, B, PAIR):
             pair = slice(a0, a0 + PAIR)
             for a in range(a0, a0 + PAIR):
                 nc.gpsimd.tensor_tensor(
@@ -137,21 +135,8 @@ def tile_clusterattention_old_kernel(
                     op=MULT,
                 )
             nc.vector.tensor_reduce(out=den[:, pair], in_=e[:, pair], axis=X, op=ADD)
+            nc.vector.reciprocal(inv_den[:, pair], den[:, pair])
             nc.vector.tensor_reduce(out=num[:, pair], in_=weighted[:, pair], axis=X, op=ADD)
-        nc.vector.reciprocal(inv_den[:, early], den[:, early])
-        late = slice(B - LAST, B)
-        for a in range(B - LAST, B):
-            for t0 in (0, T // 2):
-                half = slice(t0, t0 + T // 2)
-                nc.vector.tensor_tensor(
-                    out=weighted[:, a, half],
-                    in0=e[:, a, half],
-                    in1=val[:, a : a + 1, :].to_broadcast([P, T // 2, KEYS]),
-                    op=MULT,
-                )
-                nc.vector.tensor_reduce(out=den[:, a, half], in_=e[:, a, half], axis=X, op=ADD)
-                nc.vector.tensor_reduce(out=num[:, a, half], in_=weighted[:, a, half], axis=X, op=ADD)
-        nc.vector.reciprocal(inv_den[:, late], den[:, late])
         nc.vector.tensor_tensor(out=res[:], in0=num[:], in1=inv_den[:], op=MULT)
 
         nc.sync.dma_start(out, res[:].rearrange("h a t -> h (a t)"))

@@ -64,8 +64,8 @@ def tile_clusterattention_old_kernel(
         key_ps = psum.tile([P, B, T], F32, name="key_ps")
         val_ps = psum.tile([P, B, T], F32, name="val_ps")
         for product, weights in (
-            (q_ps, q_w_sb[:]),
             (key_ps, kv_w_sb[:, 0:P]),
+            (q_ps, q_w_sb[:]),
             (val_ps, kv_w_sb[:, P : 2 * P]),
         ):
             nc.tensor.matmul(
@@ -74,8 +74,8 @@ def tile_clusterattention_old_kernel(
         q = held.tile([P, B, T], F32, name="q")
         key = held.tile([P, B, KEYS], F32, name="key")
         val = held.tile([P, B, KEYS], F32, name="val")
-        nc.scalar.copy(key[:, :, 0:T], key_ps[:])
-        nc.scalar.copy(key[:, :, T:KEYS], blank_k_sb[:].unsqueeze(1).to_broadcast([P, B, 1]))
+        nc.vector.tensor_copy(key[:, :, 0:T], key_ps[:])
+        nc.vector.tensor_copy(key[:, :, T:KEYS], blank_k_sb[:].unsqueeze(1).to_broadcast([P, B, 1]))
         nc.scalar.copy(q[:], q_ps[:])
         nc.scalar.copy(val[:, :, 0:T], val_ps[:])
         nc.scalar.copy(val[:, :, T:KEYS], blank_v_sb[:].unsqueeze(1).to_broadcast([P, B, 1]))

@@ -80,15 +80,21 @@ def tile_clusterattention_old_kernel(
         nc.scalar.copy(val[:, :, 0:T], val_ps[:])
         nc.scalar.copy(val[:, :, T:KEYS], blank_v_sb[:].unsqueeze(1).to_broadcast([P, B, 1]))
 
-        pos = [psum.tile([P, PAIR, T, T], F32, name=f"pos{i}") for i in range(B // PAIR)]
-        for a in range(B):
-            nc.tensor.matmul(
-                pos[a // PAIR][:, a % PAIR].rearrange("h t u -> h (t u)"),
-                w_sb[:],
-                window[:].indirect(offsets[:, a * (PIECE // 16) : (a + 1) * (PIECE // 16)]),
-                start=True,
-                stop=True,
-            )
+        steps = [(a, a + 1) for a in range(2 * PAIR)] + [(a, a + PAIR) for a in range(2 * PAIR, B, PAIR)]
+        freed = {len(steps) - 2: "window_ps", len(steps) - 1: "key_ps"}
+        pos = [
+            psum.tile([P, a1 - a0, T, T], F32, name=f"pos{i}", tag=freed.get(i, f"pos{i}"))
+            for i, (a0, a1) in enumerate(steps)
+        ]
+        for i, (a0, a1) in enumerate(steps):
+            for a in range(a0, a1):
+                nc.tensor.matmul(
+                    pos[i][:, a - a0].rearrange("h t u -> h (t u)"),
+                    w_sb[:],
+                    window[:].indirect(offsets[:, a * (PIECE // 16) : (a + 1) * (PIECE // 16)]),
+                    start=True,
+                    stop=True,
+                )
 
         score = held.tile([P, B, T, KEYS], F32, name="score")
         for a in range(0, B, PAIR):
@@ -108,11 +114,10 @@ def tile_clusterattention_old_kernel(
         inv_den = held.tile([P, B, T], F32, name="inv_den")
         res = held.tile([P, B, T], F32, name="res")
 
-        steps = [(a, a + 1) for a in range(PAIR)] + [(a, a + PAIR) for a in range(PAIR, B, PAIR)]
-        for a0, a1 in steps:
+        for i, (a0, a1) in enumerate(steps):
             nc.vector.scalar_tensor_tensor(
                 out=score[:, a0:a1, :, 0:T],
-                in0=pos[a0 // PAIR][:, a0 % PAIR : a0 % PAIR + a1 - a0],
+                in0=pos[i][:],
                 scalar=pe_b_sb[:, 0:1],
                 in1=score[:, a0:a1, :, 0:T],
                 op0=ADD,

@@ -132,11 +132,12 @@ def tile_clusterattention_old_kernel(
 
         for a0 in range(0, B, PAIR):
             pair = slice(a0, a0 + PAIR)
-            for a in range(a0, a0 + PAIR):
+            samples = PAIR if a0 < B // 2 else 1
+            for a in range(a0, a0 + PAIR, samples):
                 nc.gpsimd.tensor_tensor(
-                    out=weighted[:, a],
-                    in0=e[:, a],
-                    in1=val[:, a : a + 1, :].to_broadcast([P, T, KEYS]),
+                    out=weighted[:, a : a + samples],
+                    in0=e[:, a : a + samples],
+                    in1=val[:, a : a + samples, :].unsqueeze(2).to_broadcast([P, samples, T, KEYS]),
                     op=MULT,
                 )
             nc.vector.tensor_reduce(out=den[:, pair], in_=e[:, pair], axis=X, op=ADD)

@@ -143,6 +143,10 @@ def tile_clusterattention_old_kernel(
             nc.vector.tensor_reduce(out=den[:, pair], in_=e[:, pair], axis=X, op=ADD)
             nc.vector.reciprocal(inv_den[:, pair], den[:, pair])
             nc.vector.tensor_reduce(out=num[:, pair], in_=weighted[:, pair], axis=X, op=ADD)
-        nc.vector.tensor_tensor(out=res[:], in0=num[:], in1=inv_den[:], op=MULT)
-
-        nc.sync.dma_start(out, res[:].rearrange("h a t -> h (a t)"))
+        early = slice(0, B - PAIR)
+        late = slice(B - PAIR, B)
+        for engine, part in ((nc.gpsimd, early), (nc.vector, late)):
+            engine.tensor_tensor(out=res[:, part], in0=num[:, part], in1=inv_den[:, part], op=MULT)
+            nc.sync.dma_start(
+                out[:, part.start * T : part.stop * T], res[:, part].rearrange("h a t -> h (a t)")
+            )

@@ -130,21 +130,26 @@ def tile_clusterattention_old_kernel(
                         out=e[:, a, t, :], in_=score[:, a, t, :], func=EXP, bias=neg_top[:, a, t : t + 1]
                     )
 
-        for a0 in range(0, B, PAIR):
-            pair = slice(a0, a0 + PAIR)
-            samples = PAIR if a0 < B // 2 else 1
-            for a in range(a0, a0 + PAIR, samples):
+        sums = [(a, a + PAIR) for a in range(0, B - PAIR, PAIR)] + [(B - 2, B - 1), (B - 1, B)]
+        for a0, a1 in sums:
+            if a1 <= B // 2:
+                products = [(a0, a1, 0, T)]
+            elif a1 < B:
+                products = [(a, a + 1, 0, T) for a in range(a0, a1)]
+            else:
+                products = [(a0, a1, 0, T // 2), (a0, a1, T // 2, T)]
+            for b0, b1, t0, t1 in products:
                 nc.gpsimd.tensor_tensor(
-                    out=weighted[:, a : a + samples],
-                    in0=e[:, a : a + samples],
-                    in1=val[:, a : a + samples, :].unsqueeze(2).to_broadcast([P, samples, T, KEYS]),
+                    out=weighted[:, b0:b1, t0:t1],
+                    in0=e[:, b0:b1, t0:t1],
+                    in1=val[:, b0:b1, :].unsqueeze(2).to_broadcast([P, b1 - b0, t1 - t0, KEYS]),
                     op=MULT,
                 )
-            nc.vector.tensor_reduce(out=den[:, pair], in_=e[:, pair], axis=X, op=ADD)
-            nc.vector.reciprocal(inv_den[:, pair], den[:, pair])
-            nc.vector.tensor_reduce(out=num[:, pair], in_=weighted[:, pair], axis=X, op=ADD)
-        early = slice(0, B - PAIR)
-        late = slice(B - PAIR, B)
+            nc.vector.tensor_reduce(out=den[:, a0:a1], in_=e[:, a0:a1], axis=X, op=ADD)
+            nc.vector.reciprocal(inv_den[:, a0:a1], den[:, a0:a1])
+            nc.vector.tensor_reduce(out=num[:, a0:a1], in_=weighted[:, a0:a1], axis=X, op=ADD)
+        early = slice(0, B - 1)
+        late = slice(B - 1, B)
         for engine, part in ((nc.gpsimd, early), (nc.vector, late)):
             engine.tensor_tensor(out=res[:, part], in0=num[:, part], in1=inv_den[:, part], op=MULT)
             nc.sync.dma_start(

@@ -38,9 +38,9 @@ def tile_clusterattention_old_kernel(
         pe_b_sb = held.tile([P, 1], F32, name="pe_b_sb")
         blank_k_sb = held.tile([P, 1], F32, name="blank_k_sb")
         blank_v_sb = held.tile([P, 1], F32, name="blank_v_sb")
-        nc.sync.dma_start(table_rows[:], table.rearrange("(b p) d -> p b d", p=P))
-        nc.scalar.dma_start(feat_sb[:], feat)
         nc.sync.dma_start(kv_w_sb[:], kv_w)
+        nc.scalar.dma_start(feat_sb[:], feat)
+        nc.sync.dma_start(table_rows[:], table.rearrange("(b p) d -> p b d", p=P))
         nc.scalar.dma_start(q_w_sb[:], q_w)
         nc.sync.dma_start(offsets[:], offs)
         nc.scalar.dma_start(blank_k_sb[:], blank_k)

import concourse.mybir as mybir
from concourse.masks import make_identity

BF16, F32, U16 = mybir.dt.bfloat16, mybir.dt.float32, mybir.dt.uint16
ADD, MULT, MAX = (
    mybir.AluOpType.add,
    mybir.AluOpType.mult,
    mybir.AluOpType.max,
)
EXP = mybir.ActivationFunctionType.Exp
X = mybir.AxisListType.X

P = 128
ROWS = 256
B, T = 8, 16
KEYS = T + 1
PIECE = T * T
N = B * PIECE
PAIR = 2

FLOPS = 2 * P * P * N + 2 * P * (3 * P) * (B * T)


def tile_clusterattention_old_kernel(
    tc, table, w, pe_b, feat, q_w, kv_w, blank_k, blank_v, offs, out
):
    nc = tc.nc
    with (
        tc.tile_pool(name="held", bufs=1) as held,
        tc.psum_pool(name="psum", bufs=1) as psum,
    ):
        table_rows = held.tile([P, ROWS // P, P], BF16, name="table_rows")
        offsets = held.tile([P, N // 16], U16, name="offsets")
        w_sb = held.tile([P, P], BF16, name="w_sb")
        feat_sb = held.tile([P, B * T], BF16, name="feat_sb")
        q_w_sb = held.tile([P, P], BF16, name="q_w_sb")
        kv_w_sb = held.tile([P, 2 * P], BF16, name="kv_w_sb")
        pe_b_sb = held.tile([P, 1], F32, name="pe_b_sb")
        blank_k_sb = held.tile([P, 1], F32, name="blank_k_sb")
        blank_v_sb = held.tile([P, 1], F32, name="blank_v_sb")
        nc.sync.dma_start(kv_w_sb[:], kv_w)
        nc.scalar.dma_start(feat_sb[:], feat)
        nc.sync.dma_start(table_rows[:], table.rearrange("(b p) d -> p b d", p=P))
        nc.scalar.dma_start(q_w_sb[:], q_w)
        nc.sync.dma_start(offsets[:], offs)
        nc.scalar.dma_start(blank_k_sb[:], blank_k)
        nc.sync.dma_start(w_sb[:], w)
        nc.sync.dma_start(pe_b_sb[:], pe_b)
        nc.sync.dma_start(blank_v_sb[:], blank_v)

        warm = held.tile([P, 1], F32, name="warm")
        nc.vector.memset(warm[:], 0.0)
        nc.scalar.activation(out=warm[:], in_=warm[:], func=EXP)

        ident = held.tile([P, P], BF16, name="ident")
        make_identity(nc, ident[:])
        window_ps = psum.tile([P, ROWS], BF16, name="window_ps")
        for b in range(ROWS // P):
            nc.tensor.transpose(window_ps[:, b * P : (b + 1) * P], table_rows[:, b, :], ident[:])
        window = held.tile([P, ROWS], BF16, name="window")
        nc.vector.tensor_copy(window[:], window_ps[:])

        q_ps = psum.tile([P, B, T], F32, name="q_ps")
        key_ps = psum.tile([P, B, T], F32, name="key_ps")
        val_ps = psum.tile([P, B, T], F32, name="val_ps")
        for product, weights in (
            (key_ps, kv_w_sb[:, 0:P]),
            (q_ps, q_w_sb[:]),
            (val_ps, kv_w_sb[:, P : 2 * P]),
        ):
            nc.tensor.matmul(
                product[:].rearrange("h a t -> h (a t)"), weights, feat_sb[:], start=True, stop=True
            )
        q = held.tile([P, B, T], F32, name="q")
        key = held.tile([P, B, KEYS], F32, name="key")
        val = held.tile([P, B, KEYS], F32, name="val")
        nc.vector.tensor_copy(key[:, :, 0:T], key_ps[:])
        nc.vector.tensor_copy(key[:, :, T:KEYS], blank_k_sb[:].unsqueeze(1).to_broadcast([P, B, 1]))
        nc.scalar.copy(q[:], q_ps[:])
        nc.scalar.copy(val[:, :, 0:T], val_ps[:])
        nc.scalar.copy(val[:, :, T:KEYS], blank_v_sb[:].unsqueeze(1).to_broadcast([P, B, 1]))

        steps = [(a, a + 1) for a in range(2 * PAIR)] + [(a, a + PAIR) for a in range(2 * PAIR, B, PAIR)]
        freed = {len(steps) - 2: "window_ps", len(steps) - 1: "key_ps"}
        pos = [
            psum.tile([P, a1 - a0, T, T], F32, name=f"pos{i}", tag=freed.get(i, f"pos{i}"))
            for i, (a0, a1) in enumerate(steps)
        ]
        for i, (a0, a1) in enumerate(steps):
            for a in range(a0, a1):
                nc.tensor.matmul(
                    pos[i][:, a - a0].rearrange("h t u -> h (t u)"),
                    w_sb[:],
                    window[:].indirect(offsets[:, a * (PIECE // 16) : (a + 1) * (PIECE // 16)]),
                    start=True,
                    stop=True,
                )

        score = held.tile([P, B, T, KEYS], F32, name="score")
        for a in range(0, B, PAIR):
            engine, q_of = (nc.vector, q_ps) if a == 0 else (nc.gpsimd, q)
            engine.tensor_tensor(
                out=score[:, a : a + PAIR],
                in0=q_of[:, a : a + PAIR, :].unsqueeze(3).to_broadcast([P, PAIR, T, KEYS]),
                in1=key[:, a : a + PAIR, :].unsqueeze(2).to_broadcast([P, PAIR, T, KEYS]),
                op=MULT,
            )

        neg_top = held.tile([P, B, T], F32, name="neg_top")
        e = held.tile([P, B, T, KEYS], F32, name="e")
        weighted = held.tile([P, B, T, KEYS], F32, name="weighted")
        den = held.tile([P, B, T], F32, name="den")
        num = held.tile([P, B, T], F32, name="num")
        inv_den = held.tile([P, B, T], F32, name="inv_den")
        res = held.tile([P, B, T], F32, name="res")

        for i, (a0, a1) in enumerate(steps):
            nc.vector.scalar_tensor_tensor(
                out=score[:, a0:a1, :, 0:T],
                in0=pos[i][:],
                scalar=pe_b_sb[:, 0:1],
                in1=score[:, a0:a1, :, 0:T],
                op0=ADD,
                op1=ADD,
            )
            nc.vector.tensor_reduce(out=neg_top[:, a0:a1], in_=score[:, a0:a1], axis=X, op=MAX, negate=True)
            for a in range(a0, a1):
                for t in range(T):
                    nc.scalar.activation(
                        out=e[:, a, t, :], in_=score[:, a, t, :], func=EXP, bias=neg_top[:, a, t : t + 1]
                    )

        sums = [(a, a + PAIR) for a in range(0, B - PAIR, PAIR)] + [(B - 2, B - 1), (B - 1, B)]
        for a0, a1 in sums:
            if a1 <= B // 2:
                products = [(a0, a1, 0, T)]
            elif a1 < B:
                products = [(a, a + 1, 0, T) for a in range(a0, a1)]
            else:
                products = [(a0, a1, 0, T // 2), (a0, a1, T // 2, T)]
            for b0, b1, t0, t1 in products:
                nc.gpsimd.tensor_tensor(
                    out=weighted[:, b0:b1, t0:t1],
                    in0=e[:, b0:b1, t0:t1],
                    in1=val[:, b0:b1, :].unsqueeze(2).to_broadcast([P, b1 - b0, t1 - t0, KEYS]),
                    op=MULT,
                )
            nc.vector.tensor_reduce(out=den[:, a0:a1], in_=e[:, a0:a1], axis=X, op=ADD)
            nc.vector.reciprocal(inv_den[:, a0:a1], den[:, a0:a1])
            nc.vector.tensor_reduce(out=num[:, a0:a1], in_=weighted[:, a0:a1], axis=X, op=ADD)
        early = slice(0, B - 1)
        late = slice(B - 1, B)
        for engine, part in ((nc.gpsimd, early), (nc.vector, late)):
            engine.tensor_tensor(out=res[:, part], in0=num[:, part], in1=inv_den[:, part], op=MULT)
            nc.sync.dma_start(
                out[:, part.start * T : part.stop * T], res[:, part].rearrange("h a t -> h (a t)")
            )
